import numpy as np
import ml_dtypes


def mxq(x, axis, fmt="e4m3"):
    dtype, down = {"e4m3": (ml_dtypes.float8_e4m3fn, 7), "e5m2": (ml_dtypes.float8_e5m2, 14)}[fmt]
    v = np.moveaxis(np.asarray(x, np.float32).astype(ml_dtypes.bfloat16).astype(np.float64), axis, -1)
    blocks = v.reshape(v.shape[:-1] + (-1, 32))
    amax = np.abs(blocks).max(-1, keepdims=True)
    byte = np.maximum(np.where(amax > 0, np.frexp(amax)[1] - 1 + 127, 0) - down, 1)
    scale = np.exp2(byte - 127.0)
    codes = (blocks / scale).astype(np.float32).astype(dtype).astype(np.float64)
    return np.moveaxis((codes * scale).reshape(v.shape), -1, axis)


WIDE = False


def mx_kscale(k):
    if not WIDE:
        return np.ones(k)
    levels = np.array([10, -10, 5, -5, 0])
    a = np.random.permutation(np.resize(levels, k // 512 * 4)).reshape(k // 512, 4)
    idx = np.arange(k)
    return np.exp2(a[idx // 512, idx % 128 // 32])


BF16 = ml_dtypes.bfloat16


def bf(x):
    return np.asarray(x, np.float32).astype(BF16)


def f64(x):
    return np.asarray(x).astype(np.float64)


B, S, D, N = 128, 64, 1024, 256
EPS = 1e-5


def batch_bn(x, g, b):
    m = x.mean(axis=0)
    v = x.var(axis=0)
    return g * (x - m) / np.sqrt(v + EPS) + b


def setup_inputs():
    t, u = mx_kscale(D), mx_kscale(D)
    return {"s_z2": bf(np.random.standard_normal((B, S, D)) * 0.6 + np.random.standard_normal(D) * 0.4),
            "c_z2": bf(np.random.standard_normal((B, D)) * 0.6 + np.random.standard_normal(D) * 0.4),
            "s_g2": bf((1.0 + 0.1 * np.random.standard_normal(D)) * t),
            "s_be2": bf(0.1 * np.random.standard_normal(D) * t),
            "s_w3": bf(np.random.standard_normal((N, D)) * np.sqrt(2.0 / D) / t[None, :]),
            "s_b3": bf(0.1 * np.random.standard_normal(N)),
            "c_g2": bf((1.0 + 0.1 * np.random.standard_normal(D)) * u),
            "c_be2": bf(0.1 * np.random.standard_normal(D) * u),
            "c_w3": bf(np.random.standard_normal((N, D)) * np.sqrt(2.0 / D) / u[None, :]),
            "c_b3": bf(0.1 * np.random.standard_normal(N))}


def reference(s_z2, c_z2, s_g2, s_be2, s_w3, s_b3, c_g2, c_be2, c_w3, c_b3):
    c_h = np.maximum(batch_bn(f64(c_z2), f64(c_g2), f64(c_be2)), 0.0)
    c_out = (mxq(c_h, 1, "e4m3") @ mxq(f64(c_w3), 1, "e4m3").T) + f64(c_b3)
    s_h = np.maximum(batch_bn(f64(s_z2), f64(s_g2), f64(s_be2)), 0.0)
    s_p = (mxq(s_h, 2, "e4m3") @ mxq(f64(s_w3), 1, "e4m3").T) + f64(s_b3)
    s_out = s_p * c_out[:, None, :]
    aggregated_c = s_out.max(axis=1)
    return (s_out, aggregated_c)

@@ -1,0 +1,232 @@
+from contextlib import ExitStack
+
+import concourse.mybir as mybir
+from concourse.masks import make_identity
+
+BF16 = mybir.dt.bfloat16
+F32 = mybir.dt.float32
+U32 = mybir.dt.uint32
+U8 = mybir.dt.uint8
+FP8X4 = mybir.dt.float8_e4m3fn_x4
+ACT = mybir.ActivationFunctionType
+ALU = mybir.AluOpType
+
+P = 128
+SLICES = 64
+FEATURES = 1024
+OUT = 256
+EPS = 1e-5
+CHUNKS = FEATURES // P
+PACK = 4
+PASSES = FEATURES // (P * PACK)
+GROUP = 2
+LOAD = 4
+SCALAR_EVERY = 4
+
+FLOPS = 2 * (SLICES + 1) * P * FEATURES * OUT
+
+
+def tile_cgblock_pb_t_kernel(
+    tc, s_z2, c_z2, s_g2, s_be2, s_w3, s_b3, c_g2, c_be2, c_w3, c_b3, out_0, out_1
+):
+    nc = tc.nc
+    with ExitStack() as stack:
+        const = stack.enter_context(tc.tile_pool(name="const", bufs=1))
+        small = stack.enter_context(tc.tile_pool(name="small", bufs=4))
+        work = stack.enter_context(tc.tile_pool(name="work", bufs=3))
+        results = stack.enter_context(tc.tile_pool(name="results", bufs=6))
+        psum_x = stack.enter_context(tc.psum_pool(name="psum_x", bufs=4))
+        psum_sum = stack.enter_context(tc.psum_pool(name="psum_sum", bufs=2))
+        psum_acc = stack.enter_context(tc.psum_pool(name="psum_acc", bufs=2))
+
+        ident = const.tile([P, P], BF16)
+        make_identity(nc, ident[:])
+        ones = const.tile([P, 1], BF16)
+        nc.vector.memset(ones[:], 1.0)
+        eps = const.tile([P, 1], F32)
+        nc.vector.memset(eps[:], EPS)
+        vec_rows = const.tile([P, P], BF16)
+        nc.vector.memset(vec_rows[:], 0.0)
+
+        c_x = const.tile([P, FEATURES], BF16)
+        nc.sync.dma_start(out=c_x[:], in_=c_z2)
+        for r, vec in enumerate((s_g2, s_be2, c_g2, c_be2)):
+            nc.scalar.dma_start(
+                out=vec_rows[r * CHUNKS : (r + 1) * CHUNKS, :],
+                in_=vec.rearrange("(c p) -> c p", p=P),
+            )
+        c_w_raw = const.tile([P, OUT // P, FEATURES], BF16)
+        nc.sync.dma_start(out=c_w_raw[:], in_=c_w3.rearrange("(h n) k -> n h k", n=P))
+        s_w_raw = const.tile([P, OUT // P, FEATURES], BF16)
+        nc.sync.dma_start(out=s_w_raw[:], in_=s_w3.rearrange("(h n) k -> n h k", n=P))
+        c_bias = const.tile([P, OUT], BF16)
+        nc.scalar.dma_start(out=c_bias[:], in_=c_b3.partition_broadcast(P))
+        s_bias = const.tile([P, OUT], BF16)
+        nc.scalar.dma_start(out=s_bias[:], in_=s_b3.partition_broadcast(P))
+        x_tiles = []
+        for l in range(SLICES // LOAD):
+            x_tile = const.tile([P, LOAD, FEATURES], BF16, name="x_tile%d" % l)
+            nc.sync.dma_start(out=x_tile[:], in_=s_z2[:, l * LOAD : (l + 1) * LOAD, :])
+            x_tiles.append(x_tile)
+
+        vec_t = psum_x.tile([P, CHUNKS, P], BF16, tag="xt")
+        nc.tensor.transpose(vec_t[:, 0, :], vec_rows[:], ident[:])
+        params = const.tile([P, 4, CHUNKS], F32)
+        nc.vector.tensor_copy(
+            out=params[:].rearrange("p r c -> p (r c)"), in_=vec_t[:, 0, 0 : 4 * CHUNKS]
+        )
+
+        def quantise_weight(raw, label):
+            grouped = const.tile([P, PASSES, OUT, PACK], BF16, name="%s_grouped" % label, align_bytes=64)
+            for h in range(OUT // P):
+                w_t = psum_x.tile([P, CHUNKS, P], BF16, tag="xt")
+                for c in range(CHUNKS):
+                    nc.tensor.transpose(w_t[:, c, :], raw[:, h, c * P : (c + 1) * P], ident[:])
+                for g in range(PASSES):
+                    nc.scalar.copy(
+                        out=grouped[:, g, h * P : (h + 1) * P, :],
+                        in_=w_t[:, g * PACK : (g + 1) * PACK, :].rearrange("p t n -> p n t"),
+                    )
+            codes = const.tile([P, PASSES, OUT], U32, name="%s_codes" % label, align_bytes=64)
+            scales = const.tile([P, PASSES, OUT], U8, name="%s_scales" % label, align_bytes=64)
+            nc.vector.quantize_mx(
+                out=codes[:].rearrange("p g n -> p (g n)").bitcast(FP8X4),
+                scales=scales[:].rearrange("p g n -> p (g n)"),
+                in_=grouped[:].rearrange("p g n t -> p (g n t)"),
+            )
+            return codes, scales
+
+        def hidden_to_mx(x_views, gain, shift, on_scalar):
+            n = len(x_views)
+            banks = []
+            for x in x_views:
+                x_t = psum_x.tile([P, CHUNKS, P], BF16, tag="xt")
+                for c in range(CHUNKS):
+                    nc.tensor.transpose(x_t[:, c, :], x[:, c * P : (c + 1) * P], ident[:])
+                banks.append(x_t)
+            sums = psum_sum.tile([P, GROUP, CHUNKS], F32)
+            for s, x in enumerate(x_views):
+                for c in range(CHUNKS):
+                    nc.tensor.matmul(
+                        out=sums[:, s, c : c + 1],
+                        lhsT=x[:, c * P : (c + 1) * P],
+                        rhs=ones[:],
+                        start=True,
+                        stop=True,
+                    )
+            neg_mean = small.tile([P, GROUP, CHUNKS], F32)
+            nc.vector.tensor_scalar_mul(out=neg_mean[:, :n, :], in0=sums[:, :n, :], scalar1=-1.0 / P)
+            dev2 = small.tile([P, GROUP, CHUNKS], F32)
+            for s in range(n):
+                for c in range(CHUNKS):
+                    squares = work.tile([P, P], BF16)
+                    nc.scalar.activation(
+                        out=squares[:],
+                        in_=banks[s][:, c, :],
+                        func=ACT.Square,
+                        bias=neg_mean[:, s, c : c + 1],
+                        scale=1.0,
+                        accum_out=dev2[:, s, c : c + 1],
+                    )
+            std = small.tile([P, GROUP, CHUNKS], F32)
+            nc.scalar.activation(
+                out=std[:, :n, :], in_=dev2[:, :n, :], func=ACT.Sqrt, bias=eps[:], scale=1.0 / P
+            )
+            a = small.tile([P, GROUP, CHUNKS], F32)
+            nc.vector.reciprocal(out=a[:, :n, :], in_=std[:, :n, :])
+            nc.vector.tensor_tensor(
+                out=a[:, :n, :], in0=a[:, :n, :], in1=gain.unsqueeze(1).to_broadcast([P, n, CHUNKS]), op=ALU.mult
+            )
+            b = small.tile([P, GROUP, CHUNKS], F32)
+            nc.vector.tensor_tensor(out=b[:, :n, :], in0=neg_mean[:, :n, :], in1=a[:, :n, :], op=ALU.mult)
+            nc.vector.tensor_tensor(
+                out=b[:, :n, :], in0=b[:, :n, :], in1=shift.unsqueeze(1).to_broadcast([P, n, CHUNKS]), op=ALU.add
+            )
+            planes = work.tile([P, GROUP, CHUNKS, P], BF16)
+            for s in range(n):
+                for c in range(CHUNKS):
+                    if on_scalar[s]:
+                        nc.scalar.activation(
+                            out=planes[:, s, c, :],
+                            in_=banks[s][:, c, :],
+                            func=ACT.Identity,
+                            bias=b[:, s, c : c + 1],
+                            scale=a[:, s, c : c + 1],
+                        )
+                    else:
+                        nc.vector.tensor_scalar(
+                            out=planes[:, s, c, :],
+                            in0=banks[s][:, c, :],
+                            scalar1=a[:, s, c : c + 1],
+                            scalar2=b[:, s, c : c + 1],
+                            op0=ALU.mult,
+                            op1=ALU.add,
+                        )
+            grouped = work.tile([P, GROUP, PASSES, P, PACK], BF16, align_bytes=64)
+            for s in range(n):
+                for g in range(PASSES):
+                    nc.vector.tensor_scalar_max(
+                        out=grouped[:, s, g, :, :].rearrange("p (q i) t -> p q t i", i=4),
+                        in0=planes[:, s, g * PACK : (g + 1) * PACK, :].rearrange("p t (q i) -> p q t i", i=4),
+                        scalar1=0.0,
+                    )
+            codes = work.tile([P, GROUP, PASSES, P], U32, align_bytes=64)
+            scales = work.tile([P, GROUP, PASSES, P], U8, align_bytes=64)
+            nc.vector.quantize_mx(
+                out=codes[:, :n, :, :].rearrange("p s g m -> p (s g m)").bitcast(FP8X4),
+                scales=scales[:, :n, :, :].rearrange("p s g m -> p (s g m)"),
+                in_=grouped[:, :n, :, :, :].rearrange("p s g m t -> p (s g m t)"),
+            )
+            return codes, scales
+
+        def project(acc, n, h_codes, h_scales, w_codes, w_scales):
+            for s in range(n):
+                for g in range(PASSES):
+                    nc.tensor.matmul_mx(
+                        out=acc[:, s, :],
+                        lhsT=h_codes[:, s, g, :].bitcast(FP8X4),
+                        lhsT_scale=h_scales[:, s, g, :],
+                        rhs=w_codes[:, g, :].bitcast(FP8X4),
+                        rhs_scale=w_scales[:, g, :],
+                        start=(g == 0),
+                        stop=(g == PASSES - 1),
+                    )
+
+        c_w_codes, c_w_scales = quantise_weight(c_w_raw, "c_w")
+        s_w_codes, s_w_scales = quantise_weight(s_w_raw, "s_w")
+        c_codes, c_scales = hidden_to_mx([c_x[:]], params[:, 2, :], params[:, 3, :], [False])
+        c_acc = psum_acc.tile([P, GROUP, OUT], F32, tag="acc")
+        project(c_acc, 1, c_codes, c_scales, c_w_codes, c_w_scales)
+        gate = const.tile([P, OUT], F32)
+        nc.vector.tensor_tensor(out=gate[:], in0=c_acc[:, 0, :], in1=c_bias[:], op=ALU.add)
+        gated_bias = const.tile([P, OUT], F32)
+        nc.vector.tensor_tensor(out=gated_bias[:], in0=gate[:], in1=s_bias[:], op=ALU.mult)
+
+        run_max = const.tile([P, GROUP, OUT], F32)
+        for first in range(0, SLICES, GROUP):
+            x_views = [x_tiles[i // LOAD][:, i % LOAD, :] for i in range(first, first + GROUP)]
+            on_scalar = [i % SCALAR_EVERY == SCALAR_EVERY - 1 for i in range(first, first + GROUP)]
+            h_codes, h_scales = hidden_to_mx(x_views, params[:, 0, :], params[:, 1, :], on_scalar)
+            acc = psum_acc.tile([P, GROUP, OUT], F32, tag="acc")
+            project(acc, GROUP, h_codes, h_scales, s_w_codes, s_w_scales)
+            gated = work.tile([P, GROUP, OUT], F32)
+            nc.vector.tensor_tensor(
+                out=gated[:], in0=acc[:], in1=gate[:].unsqueeze(1).to_broadcast([P, GROUP, OUT]), op=ALU.mult
+            )
+            if first == 0:
+                nc.vector.tensor_copy(out=run_max[:], in_=gated[:])
+            else:
+                nc.vector.tensor_tensor(out=run_max[:], in0=run_max[:], in1=gated[:], op=ALU.max)
+            result = results.tile([P, GROUP, OUT], F32)
+            nc.gpsimd.tensor_tensor(
+                out=result[:],
+                in0=gated[:],
+                in1=gated_bias[:].unsqueeze(1).to_broadcast([P, GROUP, OUT]),
+                op=ALU.add,
+            )
+            nc.sync.dma_start(out=out_0[:, first : first + GROUP, :], in_=result[:])
+
+        pooled = const.tile([P, OUT], F32)
+        nc.vector.tensor_tensor(out=pooled[:], in0=run_max[:, 0, :], in1=run_max[:, 1, :], op=ALU.max)
+        nc.vector.tensor_tensor(out=pooled[:], in0=pooled[:], in1=gated_bias[:], op=ALU.add)
+        nc.sync.dma_start(out=out_1, in_=pooled[:])

@@ -20,8 +20,9 @@ CHUNKS = FEATURES // P
 PACK = 4
 PASSES = FEATURES // (P * PACK)
 GROUP = 2
+JOBS = 1 + SLICES // GROUP
 LOAD = 4
-SCALAR_EVERY = 4
+HALVES = OUT // P
 
 FLOPS = 2 * (SLICES + 1) * P * FEATURES * OUT
 
@@ -31,34 +32,28 @@ def tile_cgblock_pb_t_kernel(
 ):
     nc = tc.nc
     with ExitStack() as stack:
+        stack.enter_context(tc.manual_schedule())
         const = stack.enter_context(tc.tile_pool(name="const", bufs=1))
         small = stack.enter_context(tc.tile_pool(name="small", bufs=4))
         work = stack.enter_context(tc.tile_pool(name="work", bufs=3))
         results = stack.enter_context(tc.tile_pool(name="results", bufs=6))
-        psum_x = stack.enter_context(tc.psum_pool(name="psum_x", bufs=4))
-        psum_sum = stack.enter_context(tc.psum_pool(name="psum_sum", bufs=2))
-        psum_acc = stack.enter_context(tc.psum_pool(name="psum_acc", bufs=2))
+        psum_x = stack.enter_context(tc.psum_pool(name="psum_x", bufs=6))
+        psum_sum = stack.enter_context(tc.psum_pool(name="psum_sum", bufs=1))
+        psum_acc = stack.enter_context(tc.psum_pool(name="psum_acc", bufs=1))
 
-        ident = const.tile([P, P], BF16)
-        make_identity(nc, ident[:])
-        ones = const.tile([P, 1], BF16)
-        nc.vector.memset(ones[:], 1.0)
-        eps = const.tile([P, 1], F32)
-        nc.vector.memset(eps[:], EPS)
         vec_rows = const.tile([P, P], BF16)
         nc.vector.memset(vec_rows[:], 0.0)
-
-        c_x = const.tile([P, FEATURES], BF16)
-        nc.sync.dma_start(out=c_x[:], in_=c_z2)
         for r, vec in enumerate((s_g2, s_be2, c_g2, c_be2)):
             nc.scalar.dma_start(
                 out=vec_rows[r * CHUNKS : (r + 1) * CHUNKS, :],
                 in_=vec.rearrange("(c p) -> c p", p=P),
             )
-        c_w_raw = const.tile([P, OUT // P, FEATURES], BF16)
+        c_w_raw = const.tile([P, HALVES, FEATURES], BF16)
         nc.sync.dma_start(out=c_w_raw[:], in_=c_w3.rearrange("(h n) k -> n h k", n=P))
-        s_w_raw = const.tile([P, OUT // P, FEATURES], BF16)
+        s_w_raw = const.tile([P, HALVES, FEATURES], BF16)
         nc.sync.dma_start(out=s_w_raw[:], in_=s_w3.rearrange("(h n) k -> n h k", n=P))
+        c_x = const.tile([P, FEATURES], BF16)
+        nc.sync.dma_start(out=c_x[:], in_=c_z2)
         c_bias = const.tile([P, OUT], BF16)
         nc.scalar.dma_start(out=c_bias[:], in_=c_b3.partition_broadcast(P))
         s_bias = const.tile([P, OUT], BF16)
@@ -69,6 +64,15 @@ def tile_cgblock_pb_t_kernel(
             nc.sync.dma_start(out=x_tile[:], in_=s_z2[:, l * LOAD : (l + 1) * LOAD, :])
             x_tiles.append(x_tile)
 
+        ident = const.tile([P, P], BF16)
+        make_identity(nc, ident[:])
+        ones = const.tile([P, 1], BF16)
+        nc.vector.memset(ones[:], 1.0)
+        eps = const.tile([P, 1], F32)
+        nc.vector.memset(eps[:], EPS)
+        first_sqrt = const.tile([P, 1], F32)
+        nc.scalar.activation(out=first_sqrt[:], in_=eps[:], func=ACT.Sqrt)
+
         vec_t = psum_x.tile([P, CHUNKS, P], BF16, tag="xt")
         nc.tensor.transpose(vec_t[:, 0, :], vec_rows[:], ident[:])
         params = const.tile([P, 4, CHUNKS], F32)
@@ -76,17 +80,22 @@ def tile_cgblock_pb_t_kernel(
             out=params[:].rearrange("p r c -> p (r c)"), in_=vec_t[:, 0, 0 : 4 * CHUNKS]
         )
 
-        def quantise_weight(raw, label):
+        def transpose_weight(raw, label):
             grouped = const.tile([P, PASSES, OUT, PACK], BF16, name="%s_grouped" % label, align_bytes=64)
-            for h in range(OUT // P):
+            for h in range(HALVES):
                 w_t = psum_x.tile([P, CHUNKS, P], BF16, tag="xt")
                 for c in range(CHUNKS):
                     nc.tensor.transpose(w_t[:, c, :], raw[:, h, c * P : (c + 1) * P], ident[:])
                 for g in range(PASSES):
-                    nc.scalar.copy(
-                        out=grouped[:, g, h * P : (h + 1) * P, :],
-                        in_=w_t[:, g * PACK : (g + 1) * PACK, :].rearrange("p t n -> p n t"),
-                    )
+                    dst = grouped[:, g, h * P : (h + 1) * P, :]
+                    src = w_t[:, g * PACK : (g + 1) * PACK, :].rearrange("p t n -> p n t")
+                    if h == 0:
+                        nc.vector.tensor_copy(out=dst, in_=src)
+                    else:
+                        nc.scalar.copy(out=dst, in_=src)
+            return grouped
+
+        def quantise_weight(grouped, label):
             codes = const.tile([P, PASSES, OUT], U32, name="%s_codes" % label, align_bytes=64)
             scales = const.tile([P, PASSES, OUT], U8, name="%s_scales" % label, align_bytes=64)
             nc.vector.quantize_mx(
@@ -96,16 +105,44 @@ def tile_cgblock_pb_t_kernel(
             )
             return codes, scales
 
-        def hidden_to_mx(x_views, gain, shift, on_scalar):
-            n = len(x_views)
-            banks = []
-            for x in x_views:
+        c_w_grouped = transpose_weight(c_w_raw, "c_w")
+        s_w_grouped = transpose_weight(s_w_raw, "s_w")
+        c_w = quantise_weight(c_w_grouped, "c_w")
+        s_w = quantise_weight(s_w_grouped, "s_w")
+
+        jobs = [{"x": [c_x[:]], "gain": params[:, 2, :], "shift": params[:, 3, :], "w": c_w}]
+        for first in range(0, SLICES, GROUP):
+            jobs.append(
+                {
+                    "x": [x_tiles[i // LOAD][:, i % LOAD, :] for i in range(first, first + GROUP)],
+                    "gain": params[:, 0, :],
+                    "shift": params[:, 1, :],
+                    "w": s_w,
+                    "first": first,
+                }
+            )
+        gate = const.tile([P, OUT], F32)
+        gated_bias = const.tile([P, OUT], F32)
+        run_max = const.tile([P, GROUP, OUT], F32)
+
+        def live(j):
+            return 0 <= j < JOBS
+
+        def over_slices(vec, n):
+            return vec.unsqueeze(1).to_broadcast([P, n, CHUNKS])
+
+        def transpose_and_sum(j):
+            if not live(j):
+                return
+            job = jobs[j]
+            job["banks"] = []
+            for x in job["x"]:
                 x_t = psum_x.tile([P, CHUNKS, P], BF16, tag="xt")
                 for c in range(CHUNKS):
                     nc.tensor.transpose(x_t[:, c, :], x[:, c * P : (c + 1) * P], ident[:])
-                banks.append(x_t)
+                job["banks"].append(x_t)
             sums = psum_sum.tile([P, GROUP, CHUNKS], F32)
-            for s, x in enumerate(x_views):
+            for s, x in enumerate(job["x"]):
                 for c in range(CHUNKS):
                     nc.tensor.matmul(
                         out=sums[:, s, c : c + 1],
@@ -114,17 +151,31 @@ def tile_cgblock_pb_t_kernel(
                         start=True,
                         stop=True,
                     )
+            job["sums"] = sums
+
+        def mean(j):
+            if not live(j):
+                return
+            job = jobs[j]
+            n = len(job["x"])
             neg_mean = small.tile([P, GROUP, CHUNKS], F32)
-            nc.vector.tensor_scalar_mul(out=neg_mean[:, :n, :], in0=sums[:, :n, :], scalar1=-1.0 / P)
+            nc.vector.tensor_scalar_mul(out=neg_mean[:, :n, :], in0=job["sums"][:, :n, :], scalar1=-1.0 / P)
+            job["neg_mean"] = neg_mean
+
+        def deviations(j):
+            if not live(j):
+                return
+            job = jobs[j]
+            n = len(job["x"])
             dev2 = small.tile([P, GROUP, CHUNKS], F32)
             for s in range(n):
                 for c in range(CHUNKS):
                     squares = work.tile([P, P], BF16)
                     nc.scalar.activation(
                         out=squares[:],
-                        in_=banks[s][:, c, :],
+                        in_=job["banks"][s][:, c, :],
                         func=ACT.Square,
-                        bias=neg_mean[:, s, c : c + 1],
+                        bias=job["neg_mean"][:, s, c : c + 1],
                         scale=1.0,
                         accum_out=dev2[:, s, c : c + 1],
                     )
@@ -132,99 +183,170 @@ def tile_cgblock_pb_t_kernel(
             nc.scalar.activation(
                 out=std[:, :n, :], in_=dev2[:, :n, :], func=ACT.Sqrt, bias=eps[:], scale=1.0 / P
             )
+            job["std"] = std
+
+        def inverse_std(j):
+            if not live(j):
+                return
+            job = jobs[j]
+            n = len(job["x"])
             a = small.tile([P, GROUP, CHUNKS], F32)
-            nc.vector.reciprocal(out=a[:, :n, :], in_=std[:, :n, :])
-            nc.vector.tensor_tensor(
-                out=a[:, :n, :], in0=a[:, :n, :], in1=gain.unsqueeze(1).to_broadcast([P, n, CHUNKS]), op=ALU.mult
-            )
+            nc.vector.reciprocal(out=a[:, :n, :], in_=job["std"][:, :n, :])
+            job["a"] = a
+
+        def scale(j):
+            if not live(j):
+                return
+            job = jobs[j]
+            n = len(job["x"])
+            a = job["a"]
+            nc.vector.tensor_tensor(out=a[:, :n, :], in0=a[:, :n, :], in1=over_slices(job["gain"], n), op=ALU.mult)
+
+        def mean_times_scale(j):
+            if not live(j):
+                return
+            job = jobs[j]
+            n = len(job["x"])
             b = small.tile([P, GROUP, CHUNKS], F32)
-            nc.vector.tensor_tensor(out=b[:, :n, :], in0=neg_mean[:, :n, :], in1=a[:, :n, :], op=ALU.mult)
-            nc.vector.tensor_tensor(
-                out=b[:, :n, :], in0=b[:, :n, :], in1=shift.unsqueeze(1).to_broadcast([P, n, CHUNKS]), op=ALU.add
-            )
+            nc.vector.tensor_tensor(out=b[:, :n, :], in0=job["neg_mean"][:, :n, :], in1=job["a"][:, :n, :], op=ALU.mult)
+            job["b"] = b
+
+        def shift(j):
+            if not live(j):
+                return
+            job = jobs[j]
+            n = len(job["x"])
+            b = job["b"]
+            nc.vector.tensor_tensor(out=b[:, :n, :], in0=b[:, :n, :], in1=over_slices(job["shift"], n), op=ALU.add)
+
+        def normalise(j):
+            if not live(j):
+                return
+            job = jobs[j]
             planes = work.tile([P, GROUP, CHUNKS, P], BF16)
-            for s in range(n):
+            for s in range(len(job["x"])):
                 for c in range(CHUNKS):
-                    if on_scalar[s]:
-                        nc.scalar.activation(
-                            out=planes[:, s, c, :],
-                            in_=banks[s][:, c, :],
-                            func=ACT.Identity,
-                            bias=b[:, s, c : c + 1],
-                            scale=a[:, s, c : c + 1],
-                        )
-                    else:
-                        nc.vector.tensor_scalar(
-                            out=planes[:, s, c, :],
-                            in0=banks[s][:, c, :],
-                            scalar1=a[:, s, c : c + 1],
-                            scalar2=b[:, s, c : c + 1],
-                            op0=ALU.mult,
-                            op1=ALU.add,
-                        )
-            grouped = work.tile([P, GROUP, PASSES, P, PACK], BF16, align_bytes=64)
-            for s in range(n):
-                for g in range(PASSES):
-                    nc.vector.tensor_scalar_max(
-                        out=grouped[:, s, g, :, :].rearrange("p (q i) t -> p q t i", i=4),
-                        in0=planes[:, s, g * PACK : (g + 1) * PACK, :].rearrange("p t (q i) -> p q t i", i=4),
-                        scalar1=0.0,
+                    nc.vector.tensor_scalar(
+                        out=planes[:, s, c, :],
+                        in0=job["banks"][s][:, c, :],
+                        scalar1=job["a"][:, s, c : c + 1],
+                        scalar2=job["b"][:, s, c : c + 1],
+                        op0=ALU.mult,
+                        op1=ALU.add,
                     )
+            job["planes"] = planes
+
+        def regroup_views(job, s, g):
+            dst = job["grouped"][:, s, g, :, :].rearrange("p (q i) t -> p q t i", i=4)
+            src = job["planes"][:, s, g * PACK : (g + 1) * PACK, :].rearrange("p t (q i) -> p q t i", i=4)
+            return dst, src
+
+        def blocks(job):
+            return [(s, g) for s in range(len(job["x"])) for g in range(PASSES)]
+
+        def regroup_on_vector(j):
+            if not live(j):
+                return
+            job = jobs[j]
+            grouped = work.tile([P, GROUP, PASSES, P, PACK], BF16, align_bytes=64)
+            job["grouped"] = grouped
+            for s, g in blocks(job)[:-1]:
+                dst, src = regroup_views(job, s, g)
+                nc.vector.tensor_scalar_max(out=dst, in0=src, scalar1=0.0)
+
+        def regroup_on_scalar(j):
+            if not live(j):
+                return
+            job = jobs[j]
+            s, g = blocks(job)[-1]
+            dst, src = regroup_views(job, s, g)
+            nc.scalar.activation(out=dst, in_=src, func=ACT.Relu)
+
+        def quantise(j):
+            if not live(j):
+                return
+            job = jobs[j]
+            n = len(job["x"])
             codes = work.tile([P, GROUP, PASSES, P], U32, align_bytes=64)
             scales = work.tile([P, GROUP, PASSES, P], U8, align_bytes=64)
             nc.vector.quantize_mx(
                 out=codes[:, :n, :, :].rearrange("p s g m -> p (s g m)").bitcast(FP8X4),
                 scales=scales[:, :n, :, :].rearrange("p s g m -> p (s g m)"),
-                in_=grouped[:, :n, :, :, :].rearrange("p s g m t -> p (s g m t)"),
+                in_=job["grouped"][:, :n, :, :, :].rearrange("p s g m t -> p (s g m t)"),
             )
-            return codes, scales
+            job["codes"] = codes
+            job["scales"] = scales
 
-        def project(acc, n, h_codes, h_scales, w_codes, w_scales):
-            for s in range(n):
+        def project(j):
+            if not live(j):
+                return
+            job = jobs[j]
+            w_codes, w_scales = job["w"]
+            acc = psum_acc.tile([P, GROUP, OUT], F32)
+            for s in range(len(job["x"])):
                 for g in range(PASSES):
                     nc.tensor.matmul_mx(
                         out=acc[:, s, :],
-                        lhsT=h_codes[:, s, g, :].bitcast(FP8X4),
-                        lhsT_scale=h_scales[:, s, g, :],
+                        lhsT=job["codes"][:, s, g, :].bitcast(FP8X4),
+                        lhsT_scale=job["scales"][:, s, g, :],
                         rhs=w_codes[:, g, :].bitcast(FP8X4),
                         rhs_scale=w_scales[:, g, :],
                         start=(g == 0),
                         stop=(g == PASSES - 1),
                     )
+            job["acc"] = acc
 
-        c_w_codes, c_w_scales = quantise_weight(c_w_raw, "c_w")
-        s_w_codes, s_w_scales = quantise_weight(s_w_raw, "s_w")
-        c_codes, c_scales = hidden_to_mx([c_x[:]], params[:, 2, :], params[:, 3, :], [False])
-        c_acc = psum_acc.tile([P, GROUP, OUT], F32, tag="acc")
-        project(c_acc, 1, c_codes, c_scales, c_w_codes, c_w_scales)
-        gate = const.tile([P, OUT], F32)
-        nc.vector.tensor_tensor(out=gate[:], in0=c_acc[:, 0, :], in1=c_bias[:], op=ALU.add)
-        gated_bias = const.tile([P, OUT], F32)
-        nc.vector.tensor_tensor(out=gated_bias[:], in0=gate[:], in1=s_bias[:], op=ALU.mult)
-
-        run_max = const.tile([P, GROUP, OUT], F32)
-        for first in range(0, SLICES, GROUP):
-            x_views = [x_tiles[i // LOAD][:, i % LOAD, :] for i in range(first, first + GROUP)]
-            on_scalar = [i % SCALAR_EVERY == SCALAR_EVERY - 1 for i in range(first, first + GROUP)]
-            h_codes, h_scales = hidden_to_mx(x_views, params[:, 0, :], params[:, 1, :], on_scalar)
-            acc = psum_acc.tile([P, GROUP, OUT], F32, tag="acc")
-            project(acc, GROUP, h_codes, h_scales, s_w_codes, s_w_scales)
+        def apply_gate(j):
+            if not live(j):
+                return
+            job = jobs[j]
+            if j == 0:
+                nc.vector.tensor_tensor(out=gate[:], in0=job["acc"][:, 0, :], in1=c_bias[:], op=ALU.add)
+                nc.vector.tensor_tensor(out=gated_bias[:], in0=gate[:], in1=s_bias[:], op=ALU.mult)
+                return
             gated = work.tile([P, GROUP, OUT], F32)
             nc.vector.tensor_tensor(
-                out=gated[:], in0=acc[:], in1=gate[:].unsqueeze(1).to_broadcast([P, GROUP, OUT]), op=ALU.mult
+                out=gated[:], in0=job["acc"][:], in1=gate[:].unsqueeze(1).to_broadcast([P, GROUP, OUT]), op=ALU.mult
             )
-            if first == 0:
-                nc.vector.tensor_copy(out=run_max[:], in_=gated[:])
-            else:
-                nc.vector.tensor_tensor(out=run_max[:], in0=run_max[:], in1=gated[:], op=ALU.max)
+            job["gated"] = gated
+
+        def add_bias_and_store(j):
+            if not 1 <= j < JOBS:
+                return
+            job = jobs[j]
             result = results.tile([P, GROUP, OUT], F32)
             nc.gpsimd.tensor_tensor(
                 out=result[:],
-                in0=gated[:],
+                in0=job["gated"][:],
                 in1=gated_bias[:].unsqueeze(1).to_broadcast([P, GROUP, OUT]),
                 op=ALU.add,
             )
-            nc.sync.dma_start(out=out_0[:, first : first + GROUP, :], in_=result[:])
+            nc.sync.dma_start(out=out_0[:, job["first"] : job["first"] + GROUP, :], in_=result[:])
+
+        def pool(j):
+            if not 1 <= j < JOBS:
+                return
+            if j == 1:
+                nc.vector.tensor_copy(out=run_max[:], in_=jobs[j]["gated"][:])
+            else:
+                nc.vector.tensor_tensor(out=run_max[:], in0=run_max[:], in1=jobs[j]["gated"][:], op=ALU.max)
+
+        for k in range(-2, JOBS + 3):
+            mean(k + 1)
+            regroup_on_scalar(k - 1)
+            project(k - 2)
+            inverse_std(k)
+            pool(k - 3)
+            scale(k)
+            quantise(k - 1)
+            mean_times_scale(k)
+            apply_gate(k - 2)
+            shift(k)
+            add_bias_and_store(k - 2)
+            deviations(k + 1)
+            normalise(k)
+            regroup_on_vector(k)
+            transpose_and_sum(k + 2)
 
         pooled = const.tile([P, OUT], F32)
         nc.vector.tensor_tensor(out=pooled[:], in0=run_max[:, 0, :], in1=run_max[:, 1, :], op=ALU.max)

@@ -21,7 +21,6 @@ PACK = 4
 PASSES = FEATURES // (P * PACK)
 GROUP = 2
 JOBS = 1 + SLICES // GROUP
-LOAD = 4
 HALVES = OUT // P
 
 FLOPS = 2 * (SLICES + 1) * P * FEATURES * OUT
@@ -59,9 +58,9 @@ def tile_cgblock_pb_t_kernel(
         s_bias = const.tile([P, OUT], BF16)
         nc.scalar.dma_start(out=s_bias[:], in_=s_b3.partition_broadcast(P))
         x_tiles = []
-        for l in range(SLICES // LOAD):
-            x_tile = const.tile([P, LOAD, FEATURES], BF16, name="x_tile%d" % l)
-            nc.sync.dma_start(out=x_tile[:], in_=s_z2[:, l * LOAD : (l + 1) * LOAD, :])
+        for first in range(0, SLICES, GROUP):
+            x_tile = const.tile([P, GROUP, FEATURES], BF16, name="x_tile%d" % first)
+            nc.sync.dma_start(out=x_tile[:], in_=s_z2[:, first : first + GROUP, :])
             x_tiles.append(x_tile)
 
         ident = const.tile([P, P], BF16)
@@ -70,15 +69,8 @@ def tile_cgblock_pb_t_kernel(
         nc.vector.memset(ones[:], 1.0)
         eps = const.tile([P, 1], F32)
         nc.vector.memset(eps[:], EPS)
-        first_sqrt = const.tile([P, 1], F32)
-        nc.scalar.activation(out=first_sqrt[:], in_=eps[:], func=ACT.Sqrt)
-
-        vec_t = psum_x.tile([P, CHUNKS, P], BF16, tag="xt")
-        nc.tensor.transpose(vec_t[:, 0, :], vec_rows[:], ident[:])
-        params = const.tile([P, 4, CHUNKS], F32)
-        nc.vector.tensor_copy(
-            out=params[:].rearrange("p r c -> p (r c)"), in_=vec_t[:, 0, 0 : 4 * CHUNKS]
-        )
+        first_call = const.tile([P, 1], F32)
+        nc.scalar.activation(out=first_call[:], in_=eps[:], func=ACT.Abs_reciprocal_sqrt)
 
         def transpose_weight(raw, label):
             grouped = const.tile([P, PASSES, OUT, PACK], BF16, name="%s_grouped" % label, align_bytes=64)
@@ -110,11 +102,18 @@ def tile_cgblock_pb_t_kernel(
         c_w = quantise_weight(c_w_grouped, "c_w")
         s_w = quantise_weight(s_w_grouped, "s_w")
 
+        vec_t = psum_x.tile([P, CHUNKS, P], BF16, tag="xt")
+        nc.tensor.transpose(vec_t[:, 0, :], vec_rows[:], ident[:])
+        params = const.tile([P, 4, CHUNKS], F32)
+        nc.vector.tensor_copy(
+            out=params[:].rearrange("p r c -> p (r c)"), in_=vec_t[:, 0, 0 : 4 * CHUNKS]
+        )
+
         jobs = [{"x": [c_x[:]], "gain": params[:, 2, :], "shift": params[:, 3, :], "w": c_w}]
         for first in range(0, SLICES, GROUP):
             jobs.append(
                 {
-                    "x": [x_tiles[i // LOAD][:, i % LOAD, :] for i in range(first, first + GROUP)],
+                    "x": [x_tiles[first // GROUP][:, s, :] for s in range(GROUP)],
                     "gain": params[:, 0, :],
                     "shift": params[:, 1, :],
                     "w": s_w,
@@ -179,28 +178,26 @@ def tile_cgblock_pb_t_kernel(
                         scale=1.0,
                         accum_out=dev2[:, s, c : c + 1],
                     )
-            std = small.tile([P, GROUP, CHUNKS], F32)
+            inv_std = small.tile([P, GROUP, CHUNKS], F32)
             nc.scalar.activation(
-                out=std[:, :n, :], in_=dev2[:, :n, :], func=ACT.Sqrt, bias=eps[:], scale=1.0 / P
+                out=inv_std[:, :n, :],
+                in_=dev2[:, :n, :],
+                func=ACT.Abs_reciprocal_sqrt,
+                bias=eps[:],
+                scale=1.0 / P,
             )
-            job["std"] = std
-
-        def inverse_std(j):
-            if not live(j):
-                return
-            job = jobs[j]
-            n = len(job["x"])
-            a = small.tile([P, GROUP, CHUNKS], F32)
-            nc.vector.reciprocal(out=a[:, :n, :], in_=job["std"][:, :n, :])
-            job["a"] = a
+            job["inv_std"] = inv_std
 
         def scale(j):
             if not live(j):
                 return
             job = jobs[j]
             n = len(job["x"])
-            a = job["a"]
-            nc.vector.tensor_tensor(out=a[:, :n, :], in0=a[:, :n, :], in1=over_slices(job["gain"], n), op=ALU.mult)
+            a = small.tile([P, GROUP, CHUNKS], F32)
+            nc.vector.tensor_tensor(
+                out=a[:, :n, :], in0=job["inv_std"][:, :n, :], in1=over_slices(job["gain"], n), op=ALU.mult
+            )
+            job["a"] = a
 
         def mean_times_scale(j):
             if not live(j):
@@ -305,9 +302,8 @@ def tile_cgblock_pb_t_kernel(
                 nc.vector.tensor_tensor(out=gated_bias[:], in0=gate[:], in1=s_bias[:], op=ALU.mult)
                 return
             gated = work.tile([P, GROUP, OUT], F32)
-            nc.vector.tensor_tensor(
-                out=gated[:], in0=job["acc"][:], in1=gate[:].unsqueeze(1).to_broadcast([P, GROUP, OUT]), op=ALU.mult
-            )
+            for s in range(GROUP):
+                nc.vector.tensor_tensor(out=gated[:, s, :], in0=job["acc"][:, s, :], in1=gate[:], op=ALU.mult)
             job["gated"] = gated
 
         def add_bias_and_store(j):
@@ -315,12 +311,8 @@ def tile_cgblock_pb_t_kernel(
                 return
             job = jobs[j]
             result = results.tile([P, GROUP, OUT], F32)
-            nc.gpsimd.tensor_tensor(
-                out=result[:],
-                in0=job["gated"][:],
-                in1=gated_bias[:].unsqueeze(1).to_broadcast([P, GROUP, OUT]),
-                op=ALU.add,
-            )
+            for s in range(GROUP):
+                nc.gpsimd.tensor_tensor(out=result[:, s, :], in0=job["gated"][:, s, :], in1=gated_bias[:], op=ALU.add)
             nc.sync.dma_start(out=out_0[:, job["first"] : job["first"] + GROUP, :], in_=result[:])
 
         def pool(j):
@@ -335,13 +327,12 @@ def tile_cgblock_pb_t_kernel(
             mean(k + 1)
             regroup_on_scalar(k - 1)
             project(k - 2)
-            inverse_std(k)
-            pool(k - 3)
             scale(k)
-            quantise(k - 1)
+            pool(k - 3)
             mean_times_scale(k)
-            apply_gate(k - 2)
+            quantise(k - 1)
             shift(k)
+            apply_gate(k - 2)
             add_bias_and_store(k - 2)
             deviations(k + 1)
             normalise(k)

@@ -70,17 +70,22 @@ def tile_cgblock_pb_t_kernel(
         eps = const.tile([P, 1], F32)
         nc.vector.memset(eps[:], EPS)
         first_call = const.tile([P, 1], F32)
-        nc.scalar.activation(out=first_call[:], in_=eps[:], func=ACT.Abs_reciprocal_sqrt)
+        nc.scalar.activation(out=first_call[:], in_=eps[:], func=ACT.Sqrt)
 
         def transpose_weight(raw, label):
             grouped = const.tile([P, PASSES, OUT, PACK], BF16, name="%s_grouped" % label, align_bytes=64)
+            banks = []
             for h in range(HALVES):
                 w_t = psum_x.tile([P, CHUNKS, P], BF16, tag="xt")
-                for c in range(CHUNKS):
-                    nc.tensor.transpose(w_t[:, c, :], raw[:, h, c * P : (c + 1) * P], ident[:])
+                banks.append(w_t)
+            for g in range(PASSES):
+                for h in range(HALVES):
+                    for c in range(g * PACK, (g + 1) * PACK):
+                        nc.tensor.transpose(banks[h][:, c, :], raw[:, h, c * P : (c + 1) * P], ident[:])
+            for h in range(HALVES):
                 for g in range(PASSES):
                     dst = grouped[:, g, h * P : (h + 1) * P, :]
-                    src = w_t[:, g * PACK : (g + 1) * PACK, :].rearrange("p t n -> p n t")
+                    src = banks[h][:, g * PACK : (g + 1) * PACK, :].rearrange("p t n -> p n t")
                     if h == 0:
                         nc.vector.tensor_copy(out=dst, in_=src)
                     else:
@@ -137,9 +142,11 @@ def tile_cgblock_pb_t_kernel(
             job["banks"] = []
             for x in job["x"]:
                 x_t = psum_x.tile([P, CHUNKS, P], BF16, tag="xt")
-                for c in range(CHUNKS):
-                    nc.tensor.transpose(x_t[:, c, :], x[:, c * P : (c + 1) * P], ident[:])
                 job["banks"].append(x_t)
+            for g in range(PASSES):
+                for x, x_t in zip(job["x"], job["banks"]):
+                    for c in range(g * PACK, (g + 1) * PACK):
+                        nc.tensor.transpose(x_t[:, c, :], x[:, c * P : (c + 1) * P], ident[:])
             sums = psum_sum.tile([P, GROUP, CHUNKS], F32)
             for s, x in enumerate(job["x"]):
                 for c in range(CHUNKS):
@@ -158,7 +165,7 @@ def tile_cgblock_pb_t_kernel(
             job = jobs[j]
             n = len(job["x"])
             neg_mean = small.tile([P, GROUP, CHUNKS], F32)
-            nc.vector.tensor_scalar_mul(out=neg_mean[:, :n, :], in0=job["sums"][:, :n, :], scalar1=-1.0 / P)
+            nc.scalar.mul(out=neg_mean[:, :n, :], in_=job["sums"][:, :n, :], mul=-1.0 / P)
             job["neg_mean"] = neg_mean
 
         def deviations(j):
@@ -178,26 +185,28 @@ def tile_cgblock_pb_t_kernel(
                         scale=1.0,
                         accum_out=dev2[:, s, c : c + 1],
                     )
-            inv_std = small.tile([P, GROUP, CHUNKS], F32)
+            std = small.tile([P, GROUP, CHUNKS], F32)
             nc.scalar.activation(
-                out=inv_std[:, :n, :],
-                in_=dev2[:, :n, :],
-                func=ACT.Abs_reciprocal_sqrt,
-                bias=eps[:],
-                scale=1.0 / P,
+                out=std[:, :n, :], in_=dev2[:, :n, :], func=ACT.Sqrt, bias=eps[:], scale=1.0 / P
             )
-            job["inv_std"] = inv_std
+            job["std"] = std
+
+        def inverse_std(j):
+            if not live(j):
+                return
+            job = jobs[j]
+            n = len(job["x"])
+            a = small.tile([P, GROUP, CHUNKS], F32)
+            nc.vector.reciprocal(out=a[:, :n, :], in_=job["std"][:, :n, :])
+            job["a"] = a
 
         def scale(j):
             if not live(j):
                 return
             job = jobs[j]
             n = len(job["x"])
-            a = small.tile([P, GROUP, CHUNKS], F32)
-            nc.vector.tensor_tensor(
-                out=a[:, :n, :], in0=job["inv_std"][:, :n, :], in1=over_slices(job["gain"], n), op=ALU.mult
-            )
-            job["a"] = a
+            a = job["a"]
+            nc.vector.tensor_tensor(out=a[:, :n, :], in0=a[:, :n, :], in1=over_slices(job["gain"], n), op=ALU.mult)
 
         def mean_times_scale(j):
             if not live(j):
@@ -293,18 +302,20 @@ def tile_cgblock_pb_t_kernel(
                     )
             job["acc"] = acc
 
-        def apply_gate(j):
+        def apply_gate(j, s):
             if not live(j):
                 return
             job = jobs[j]
             if j == 0:
-                nc.vector.tensor_tensor(out=gate[:], in0=job["acc"][:, 0, :], in1=c_bias[:], op=ALU.add)
-                nc.vector.tensor_tensor(out=gated_bias[:], in0=gate[:], in1=s_bias[:], op=ALU.mult)
+                if s == 0:
+                    nc.vector.tensor_tensor(out=gate[:], in0=job["acc"][:, 0, :], in1=c_bias[:], op=ALU.add)
+                else:
+                    nc.vector.tensor_tensor(out=gated_bias[:], in0=gate[:], in1=s_bias[:], op=ALU.mult)
                 return
-            gated = work.tile([P, GROUP, OUT], F32)
-            for s in range(GROUP):
-                nc.vector.tensor_tensor(out=gated[:, s, :], in0=job["acc"][:, s, :], in1=gate[:], op=ALU.mult)
-            job["gated"] = gated
+            if s == 0:
+                gated = work.tile([P, GROUP, OUT], F32)
+                job["gated"] = gated
+            nc.vector.tensor_tensor(out=job["gated"][:, s, :], in0=job["acc"][:, s, :], in1=gate[:], op=ALU.mult)
 
         def add_bias_and_store(j):
             if not 1 <= j < JOBS:
@@ -324,20 +335,22 @@ def tile_cgblock_pb_t_kernel(
                 nc.vector.tensor_tensor(out=run_max[:], in0=run_max[:], in1=jobs[j]["gated"][:], op=ALU.max)
 
         for k in range(-2, JOBS + 3):
-            mean(k + 1)
-            regroup_on_scalar(k - 1)
             project(k - 2)
-            scale(k)
+            inverse_std(k)
             pool(k - 3)
-            mean_times_scale(k)
+            scale(k)
             quantise(k - 1)
+            mean_times_scale(k)
+            apply_gate(k - 2, 0)
             shift(k)
-            apply_gate(k - 2)
+            apply_gate(k - 2, 1)
             add_bias_and_store(k - 2)
             deviations(k + 1)
             normalise(k)
             regroup_on_vector(k)
             transpose_and_sum(k + 2)
+            mean(k + 2)
+            regroup_on_scalar(k)
 
         pooled = const.tile([P, OUT], F32)
         nc.vector.tensor_tensor(out=pooled[:], in0=run_max[:, 0, :], in1=run_max[:, 1, :], op=ALU.max)

from contextlib import ExitStack

import concourse.mybir as mybir
from concourse.masks import make_identity

BF16 = mybir.dt.bfloat16
F32 = mybir.dt.float32
U32 = mybir.dt.uint32
U8 = mybir.dt.uint8
FP8X4 = mybir.dt.float8_e4m3fn_x4
ACT = mybir.ActivationFunctionType
ALU = mybir.AluOpType

P = 128
SLICES = 64
FEATURES = 1024
OUT = 256
EPS = 1e-5
CHUNKS = FEATURES // P
PACK = 4
PASSES = FEATURES // (P * PACK)
GROUP = 2
JOBS = 1 + SLICES // GROUP
HALVES = OUT // P

FLOPS = 2 * (SLICES + 1) * P * FEATURES * OUT


def tile_cgblock_pb_t_kernel(
    tc, s_z2, c_z2, s_g2, s_be2, s_w3, s_b3, c_g2, c_be2, c_w3, c_b3, out_0, out_1
):
    nc = tc.nc
    with ExitStack() as stack:
        stack.enter_context(tc.manual_schedule())
        const = stack.enter_context(tc.tile_pool(name="const", bufs=1))
        small = stack.enter_context(tc.tile_pool(name="small", bufs=4))
        work = stack.enter_context(tc.tile_pool(name="work", bufs=3))
        results = stack.enter_context(tc.tile_pool(name="results", bufs=6))
        psum_x = stack.enter_context(tc.psum_pool(name="psum_x", bufs=6))
        psum_sum = stack.enter_context(tc.psum_pool(name="psum_sum", bufs=1))
        psum_acc = stack.enter_context(tc.psum_pool(name="psum_acc", bufs=1))

        vec_rows = const.tile([P, P], BF16)
        nc.vector.memset(vec_rows[:], 0.0)
        for r, vec in enumerate((s_g2, s_be2, c_g2, c_be2)):
            nc.scalar.dma_start(
                out=vec_rows[r * CHUNKS : (r + 1) * CHUNKS, :],
                in_=vec.rearrange("(c p) -> c p", p=P),
            )
        c_w_raw = const.tile([P, HALVES, FEATURES], BF16)
        nc.sync.dma_start(out=c_w_raw[:], in_=c_w3.rearrange("(h n) k -> n h k", n=P))
        s_w_raw = const.tile([P, HALVES, FEATURES], BF16)
        nc.sync.dma_start(out=s_w_raw[:], in_=s_w3.rearrange("(h n) k -> n h k", n=P))
        c_x = const.tile([P, FEATURES], BF16)
        nc.sync.dma_start(out=c_x[:], in_=c_z2)
        c_bias = const.tile([P, OUT], BF16)
        nc.scalar.dma_start(out=c_bias[:], in_=c_b3.partition_broadcast(P))
        s_bias = const.tile([P, OUT], BF16)
        nc.scalar.dma_start(out=s_bias[:], in_=s_b3.partition_broadcast(P))
        x_tiles = []
        for first in range(0, SLICES, GROUP):
            x_tile = const.tile([P, GROUP, FEATURES], BF16, name="x_tile%d" % first)
            nc.sync.dma_start(out=x_tile[:], in_=s_z2[:, first : first + GROUP, :])
            x_tiles.append(x_tile)

        ident = const.tile([P, P], BF16)
        make_identity(nc, ident[:])
        ones = const.tile([P, 1], BF16)
        nc.vector.memset(ones[:], 1.0)
        eps = const.tile([P, 1], F32)
        nc.vector.memset(eps[:], EPS)
        first_call = const.tile([P, 1], F32)
        nc.scalar.activation(out=first_call[:], in_=eps[:], func=ACT.Sqrt)

        def transpose_weight(raw, label):
            grouped = const.tile([P, PASSES, OUT, PACK], BF16, name="%s_grouped" % label, align_bytes=64)
            banks = []
            for h in range(HALVES):
                w_t = psum_x.tile([P, CHUNKS, P], BF16, tag="xt")
                banks.append(w_t)
            for g in range(PASSES):
                for h in range(HALVES):
                    for c in range(g * PACK, (g + 1) * PACK):
                        nc.tensor.transpose(banks[h][:, c, :], raw[:, h, c * P : (c + 1) * P], ident[:])
            for h in range(HALVES):
                for g in range(PASSES):
                    dst = grouped[:, g, h * P : (h + 1) * P, :]
                    src = banks[h][:, g * PACK : (g + 1) * PACK, :].rearrange("p t n -> p n t")
                    if h == 0:
                        nc.vector.tensor_copy(out=dst, in_=src)
                    else:
                        nc.scalar.copy(out=dst, in_=src)
            return grouped

        def quantise_weight(grouped, label):
            codes = const.tile([P, PASSES, OUT], U32, name="%s_codes" % label, align_bytes=64)
            scales = const.tile([P, PASSES, OUT], U8, name="%s_scales" % label, align_bytes=64)
            nc.vector.quantize_mx(
                out=codes[:].rearrange("p g n -> p (g n)").bitcast(FP8X4),
                scales=scales[:].rearrange("p g n -> p (g n)"),
                in_=grouped[:].rearrange("p g n t -> p (g n t)"),
            )
            return codes, scales

        c_w_grouped = transpose_weight(c_w_raw, "c_w")
        s_w_grouped = transpose_weight(s_w_raw, "s_w")
        c_w = quantise_weight(c_w_grouped, "c_w")
        s_w = quantise_weight(s_w_grouped, "s_w")

        vec_t = psum_x.tile([P, CHUNKS, P], BF16, tag="xt")
        nc.tensor.transpose(vec_t[:, 0, :], vec_rows[:], ident[:])
        params = const.tile([P, 4, CHUNKS], F32)
        nc.vector.tensor_copy(
            out=params[:].rearrange("p r c -> p (r c)"), in_=vec_t[:, 0, 0 : 4 * CHUNKS]
        )

        jobs = [{"x": [c_x[:]], "gain": params[:, 2, :], "shift": params[:, 3, :], "w": c_w}]
        for first in range(0, SLICES, GROUP):
            jobs.append(
                {
                    "x": [x_tiles[first // GROUP][:, s, :] for s in range(GROUP)],
                    "gain": params[:, 0, :],
                    "shift": params[:, 1, :],
                    "w": s_w,
                    "first": first,
                }
            )
        gate = const.tile([P, OUT], F32)
        gated_bias = const.tile([P, OUT], F32)
        run_max = const.tile([P, GROUP, OUT], F32)

        def live(j):
            return 0 <= j < JOBS

        def over_slices(vec, n):
            return vec.unsqueeze(1).to_broadcast([P, n, CHUNKS])

        def transpose_and_sum(j):
            if not live(j):
                return
            job = jobs[j]
            job["banks"] = []
            for x in job["x"]:
                x_t = psum_x.tile([P, CHUNKS, P], BF16, tag="xt")
                job["banks"].append(x_t)
            for g in range(PASSES):
                for x, x_t in zip(job["x"], job["banks"]):
                    for c in range(g * PACK, (g + 1) * PACK):
                        nc.tensor.transpose(x_t[:, c, :], x[:, c * P : (c + 1) * P], ident[:])
            sums = psum_sum.tile([P, GROUP, CHUNKS], F32)
            for s, x in enumerate(job["x"]):
                for c in range(CHUNKS):
                    nc.tensor.matmul(
                        out=sums[:, s, c : c + 1],
                        lhsT=x[:, c * P : (c + 1) * P],
                        rhs=ones[:],
                        start=True,
                        stop=True,
                    )
            job["sums"] = sums

        def mean(j):
            if not live(j):
                return
            job = jobs[j]
            n = len(job["x"])
            neg_mean = small.tile([P, GROUP, CHUNKS], F32)
            nc.scalar.mul(out=neg_mean[:, :n, :], in_=job["sums"][:, :n, :], mul=-1.0 / P)
            job["neg_mean"] = neg_mean

        def deviations(j):
            if not live(j):
                return
            job = jobs[j]
            n = len(job["x"])
            dev2 = small.tile([P, GROUP, CHUNKS], F32)
            for s in range(n):
                for c in range(CHUNKS):
                    squares = work.tile([P, P], BF16)
                    nc.scalar.activation(
                        out=squares[:],
                        in_=job["banks"][s][:, c, :],
                        func=ACT.Square,
                        bias=job["neg_mean"][:, s, c : c + 1],
                        scale=1.0,
                        accum_out=dev2[:, s, c : c + 1],
                    )
            std = small.tile([P, GROUP, CHUNKS], F32)
            nc.scalar.activation(
                out=std[:, :n, :], in_=dev2[:, :n, :], func=ACT.Sqrt, bias=eps[:], scale=1.0 / P
            )
            job["std"] = std

        def inverse_std(j):
            if not live(j):
                return
            job = jobs[j]
            n = len(job["x"])
            a = small.tile([P, GROUP, CHUNKS], F32)
            nc.vector.reciprocal(out=a[:, :n, :], in_=job["std"][:, :n, :])
            job["a"] = a

        def scale(j):
            if not live(j):
                return
            job = jobs[j]
            n = len(job["x"])
            a = job["a"]
            nc.vector.tensor_tensor(out=a[:, :n, :], in0=a[:, :n, :], in1=over_slices(job["gain"], n), op=ALU.mult)

        def mean_times_scale(j):
            if not live(j):
                return
            job = jobs[j]
            n = len(job["x"])
            b = small.tile([P, GROUP, CHUNKS], F32)
            nc.vector.tensor_tensor(out=b[:, :n, :], in0=job["neg_mean"][:, :n, :], in1=job["a"][:, :n, :], op=ALU.mult)
            job["b"] = b

        def shift(j):
            if not live(j):
                return
            job = jobs[j]
            n = len(job["x"])
            b = job["b"]
            nc.vector.tensor_tensor(out=b[:, :n, :], in0=b[:, :n, :], in1=over_slices(job["shift"], n), op=ALU.add)

        def normalise(j):
            if not live(j):
                return
            job = jobs[j]
            planes = work.tile([P, GROUP, CHUNKS, P], BF16)
            for s in range(len(job["x"])):
                for c in range(CHUNKS):
                    nc.vector.tensor_scalar(
                        out=planes[:, s, c, :],
                        in0=job["banks"][s][:, c, :],
                        scalar1=job["a"][:, s, c : c + 1],
                        scalar2=job["b"][:, s, c : c + 1],
                        op0=ALU.mult,
                        op1=ALU.add,
                    )
            job["planes"] = planes

        def regroup_views(job, s, g):
            dst = job["grouped"][:, s, g, :, :].rearrange("p (q i) t -> p q t i", i=4)
            src = job["planes"][:, s, g * PACK : (g + 1) * PACK, :].rearrange("p t (q i) -> p q t i", i=4)
            return dst, src

        def blocks(job):
            return [(s, g) for s in range(len(job["x"])) for g in range(PASSES)]

        def regroup_on_vector(j):
            if not live(j):
                return
            job = jobs[j]
            grouped = work.tile([P, GROUP, PASSES, P, PACK], BF16, align_bytes=64)
            job["grouped"] = grouped
            for s, g in blocks(job)[:-1]:
                dst, src = regroup_views(job, s, g)
                nc.vector.tensor_scalar_max(out=dst, in0=src, scalar1=0.0)

        def regroup_on_scalar(j):
            if not live(j):
                return
            job = jobs[j]
            s, g = blocks(job)[-1]
            dst, src = regroup_views(job, s, g)
            nc.scalar.activation(out=dst, in_=src, func=ACT.Relu)

        def quantise(j):
            if not live(j):
                return
            job = jobs[j]
            n = len(job["x"])
            codes = work.tile([P, GROUP, PASSES, P], U32, align_bytes=64)
            scales = work.tile([P, GROUP, PASSES, P], U8, align_bytes=64)
            nc.vector.quantize_mx(
                out=codes[:, :n, :, :].rearrange("p s g m -> p (s g m)").bitcast(FP8X4),
                scales=scales[:, :n, :, :].rearrange("p s g m -> p (s g m)"),
                in_=job["grouped"][:, :n, :, :, :].rearrange("p s g m t -> p (s g m t)"),
            )
            job["codes"] = codes
            job["scales"] = scales

        def project(j):
            if not live(j):
                return
            job = jobs[j]
            w_codes, w_scales = job["w"]
            acc = psum_acc.tile([P, GROUP, OUT], F32)
            for s in range(len(job["x"])):
                for g in range(PASSES):
                    nc.tensor.matmul_mx(
                        out=acc[:, s, :],
                        lhsT=job["codes"][:, s, g, :].bitcast(FP8X4),
                        lhsT_scale=job["scales"][:, s, g, :],
                        rhs=w_codes[:, g, :].bitcast(FP8X4),
                        rhs_scale=w_scales[:, g, :],
                        start=(g == 0),
                        stop=(g == PASSES - 1),
                    )
            job["acc"] = acc

        def apply_gate(j, s):
            if not live(j):
                return
            job = jobs[j]
            if j == 0:
                if s == 0:
                    nc.vector.tensor_tensor(out=gate[:], in0=job["acc"][:, 0, :], in1=c_bias[:], op=ALU.add)
                else:
                    nc.vector.tensor_tensor(out=gated_bias[:], in0=gate[:], in1=s_bias[:], op=ALU.mult)
                return
            if s == 0:
                gated = work.tile([P, GROUP, OUT], F32)
                job["gated"] = gated
            nc.vector.tensor_tensor(out=job["gated"][:, s, :], in0=job["acc"][:, s, :], in1=gate[:], op=ALU.mult)

        def add_bias_and_store(j):
            if not 1 <= j < JOBS:
                return
            job = jobs[j]
            result = results.tile([P, GROUP, OUT], F32)
            for s in range(GROUP):
                nc.gpsimd.tensor_tensor(out=result[:, s, :], in0=job["gated"][:, s, :], in1=gated_bias[:], op=ALU.add)
            nc.sync.dma_start(out=out_0[:, job["first"] : job["first"] + GROUP, :], in_=result[:])

        def pool(j):
            if not 1 <= j < JOBS:
                return
            if j == 1:
                nc.vector.tensor_copy(out=run_max[:], in_=jobs[j]["gated"][:])
            else:
                nc.vector.tensor_tensor(out=run_max[:], in0=run_max[:], in1=jobs[j]["gated"][:], op=ALU.max)

        for k in range(-2, JOBS + 3):
            project(k - 2)
            inverse_std(k)
            pool(k - 3)
            scale(k)
            quantise(k - 1)
            mean_times_scale(k)
            apply_gate(k - 2, 0)
            shift(k)
            apply_gate(k - 2, 1)
            add_bias_and_store(k - 2)
            deviations(k + 1)
            normalise(k)
            regroup_on_vector(k)
            transpose_and_sum(k + 2)
            mean(k + 2)
            regroup_on_scalar(k)

        pooled = const.tile([P, OUT], F32)
        nc.vector.tensor_tensor(out=pooled[:], in0=run_max[:, 0, :], in1=run_max[:, 1, :], op=ALU.max)
        nc.vector.tensor_tensor(out=pooled[:], in0=pooled[:], in1=gated_bias[:], op=ALU.add)
        nc.sync.dma_start(out=out_1, in_=pooled[:])
